import numpy as np
import ml_dtypes


def mxq(x, axis, fmt="e4m3"):
    dtype, down = {"e4m3": (ml_dtypes.float8_e4m3fn, 7), "e5m2": (ml_dtypes.float8_e5m2, 14)}[fmt]
    v = np.moveaxis(np.asarray(x, np.float32).astype(ml_dtypes.bfloat16).astype(np.float64), axis, -1)
    blocks = v.reshape(v.shape[:-1] + (-1, 32))
    amax = np.abs(blocks).max(-1, keepdims=True)
    byte = np.maximum(np.where(amax > 0, np.frexp(amax)[1] - 1 + 127, 0) - down, 1)
    scale = np.exp2(byte - 127.0)
    codes = (blocks / scale).astype(np.float32).astype(dtype).astype(np.float64)
    return np.moveaxis((codes * scale).reshape(v.shape), -1, axis)


WIDE = False


def mx_kscale(k):
    if not WIDE:
        return np.ones(k)
    levels = np.array([10, -10, 5, -5, 0])
    a = np.random.permutation(np.resize(levels, k // 512 * 4)).reshape(k // 512, 4)
    idx = np.arange(k)
    return np.exp2(a[idx // 512, idx % 128 // 32])


BF16 = ml_dtypes.bfloat16


def bf(x):
    return np.asarray(x, np.float32).astype(BF16)


def f64(x):
    return np.asarray(x).astype(np.float64)


E, B, STATE, ACTION, H0, H1, H2, H3 = 7, 256, 128, 8, 256, 256, 512, 512


def swish(v):
    return v * (1.0 / (1.0 + np.exp(-v)))


def softplus(v):
    return np.maximum(v, 0.0) + np.log(1.0 + np.exp(-np.abs(v)))


def soft_clamp(x, lo, hi):
    x = hi - softplus(hi - x)
    x = lo + softplus(x - lo)
    return x


def setup_inputs():
    s = mx_kscale(H2)
    return {
        "h2": bf(swish(np.random.standard_normal((E, B, H2))) * s),
        "W3": bf(np.random.standard_normal((E, H2, H3)) * 1.5 / np.sqrt(H2) / s[None, :, None]),
        "b3": bf(np.random.standard_normal((E, H3)) * 0.2),
        "Wmu": bf(np.random.standard_normal((E, H3, STATE)) * 1.5 / np.sqrt(H3)),
        "bmu": bf(np.random.standard_normal((E, STATE)) * 0.2),
        "Wsig": bf(np.random.standard_normal((E, H3, STATE)) * 2.5 / np.sqrt(H3)),
        "bsig": bf(np.random.standard_normal((E, STATE)) * 0.2),
        "max_logstd": bf(1.0 + 0.2 * np.random.standard_normal(STATE)),
        "min_logstd": bf(-1.0 + 0.2 * np.random.standard_normal(STATE)),
        "state": bf(np.random.standard_normal((B, STATE))),
    }


def reference(h2, W3, b3, Wmu, bmu, Wsig, bsig, max_logstd, min_logstd, state):
    h = swish((mxq(f64(h2), 2, "e4m3") @ mxq(f64(W3), 1, "e4m3")) + f64(b3)[:, None, :])
    hq = mxq(h, 2, "e4m3")
    mu = (hq @ mxq(f64(Wmu), 1, "e4m3")) + f64(bmu)[:, None, :]
    log_sigma = (hq @ mxq(f64(Wsig), 1, "e4m3")) + f64(bsig)[:, None, :]
    log_sigma = soft_clamp(log_sigma, f64(min_logstd), f64(max_logstd))
    sigma = np.exp(log_sigma)
    mu = mu + f64(state)[None, :, :]
    return mu, sigma

@@ -1,0 +1,313 @@
+from contextlib import ExitStack
+
+import concourse.mybir as mybir
+from concourse.masks import make_identity
+
+F32 = mybir.dt.float32
+BF16 = mybir.dt.bfloat16
+U32 = mybir.dt.uint32
+U8 = mybir.dt.uint8
+FP8X4 = mybir.dt.float8_e4m3fn_x4
+ACT = mybir.ActivationFunctionType
+ALU = mybir.AluOpType
+
+P = 128
+PACK = 4
+E = 7
+B = 256
+ROWS = B // P
+H2 = 512
+H3 = 512
+S = 128
+RUN = 4
+
+ROW_B3 = 0
+ROW_BMU = ROW_B3 + E * PACK
+ROW_BSIG = ROW_BMU + E
+ROW_MAX = ROW_BSIG + E
+ROW_MIN = ROW_MAX + 1
+
+FLOPS = 2 * E * B * (H2 * H3 + 2 * H3 * S)
+
+
+def regroup(copy, grouped, planes):
+    copy(
+        out=grouped.rearrange("p (m i) t -> p m t i", i=RUN),
+        in_=planes.rearrange("p t (m i) -> p m t i", i=RUN),
+    )
+
+
+def tile_ensembledynamicmodel_pa_kernel(
+    tc, h2, W3, b3, Wmu, bmu, Wsig, bsig, max_logstd, min_logstd, state, out_0, out_1
+):
+    nc = tc.nc
+    with ExitStack() as ctx:
+        const = ctx.enter_context(tc.tile_pool(name="const", bufs=1))
+        inputs = ctx.enter_context(tc.tile_pool(name="inputs", bufs=1))
+        work = ctx.enter_context(tc.tile_pool(name="work", bufs=3))
+        results = ctx.enter_context(tc.tile_pool(name="results", bufs=E))
+        psum = ctx.enter_context(tc.psum_pool(name="psum", bufs=1))
+        small_rows = const.tile([P, P], BF16)
+        nc.vector.memset(small_rows[:], 0.0)
+        nc.scalar.dma_start(
+            out=small_rows[ROW_B3:ROW_BMU, :], in_=b3.rearrange("e (t p) -> (e t) p", p=P)
+        )
+        nc.scalar.dma_start(out=small_rows[ROW_BMU:ROW_BSIG, :], in_=bmu)
+        nc.scalar.dma_start(out=small_rows[ROW_BSIG:ROW_MAX, :], in_=bsig)
+        nc.scalar.dma_start(
+            out=small_rows[ROW_MAX:ROW_MIN, :], in_=max_logstd.rearrange("(o s) -> o s", o=1)
+        )
+        nc.scalar.dma_start(
+            out=small_rows[ROW_MIN : ROW_MIN + 1, :], in_=min_logstd.rearrange("(o s) -> o s", o=1)
+        )
+        state_rows = const.tile([P, ROWS, S], BF16)
+        nc.scalar.dma_start(out=state_rows[:], in_=state.rearrange("(p c) s -> p c s", c=ROWS))
+
+        h2_rows = {}
+        w3_planes = {}
+        heads_planes = {}
+        for e in range(E):
+            h2_in = inputs.tile([P, ROWS, H2], BF16, name="h2_rows%d" % e)
+            nc.sync.dma_start(out=h2_in[:], in_=h2[e].rearrange("(p c) k -> p c k", c=ROWS))
+            h2_rows[e] = h2_in
+            w3_in = inputs.tile([P, PACK, H3], BF16, name="w3_planes%d" % e)
+            nc.sync.dma_start(
+                out=w3_in[:].rearrange("q (u r) n -> q u (r n)", u=2),
+                in_=W3[e].rearrange("(u q r) n -> q u (r n)", u=2, r=2),
+            )
+            w3_planes[e] = w3_in
+            heads_in = inputs.tile([P, PACK, 2 * S], BF16, name="heads_planes%d" % e)
+            nc.sync.dma_start(
+                out=heads_in[:, :, 0:S], in_=Wmu[e].rearrange("(t p) s -> p t s", p=P)
+            )
+            nc.sync.dma_start(
+                out=heads_in[:, :, S : 2 * S], in_=Wsig[e].rearrange("(t p) s -> p t s", p=P)
+            )
+            heads_planes[e] = heads_in
+
+        identity = const.tile([P, P], F32)
+        make_identity(nc, identity[:])
+
+        h2_words = {}
+        h2_grouped = {}
+        h2_mx = {}
+        w3_grouped = {}
+        w3_mx = {}
+        heads_grouped = {}
+        heads_mx = {}
+        hidden_sums = {}
+        h_grouped = {}
+        h_mx = {}
+        head_sums = {}
+        turned = {}
+        turned_back = {}
+
+        def quantise(grouped, width, label):
+            codes = work.tile([P, width], U32, name=label + "_codes", align_bytes=64)
+            scales = work.tile([P, width], U8, name=label + "_scales", align_bytes=64)
+            nc.vector.quantize_mx(
+                out=codes[:].bitcast(FP8X4),
+                scales=scales[:],
+                in_=grouped[:].rearrange("p w t -> p (w t)"),
+            )
+            return codes, scales
+
+        def multiply(out, stationary, chunk, moving):
+            nc.tensor.matmul_mx(
+                out=out,
+                lhsT=stationary[0][:, chunk].bitcast(FP8X4),
+                lhsT_scale=stationary[1][:, chunk],
+                rhs=moving[0][:].bitcast(FP8X4),
+                rhs_scale=moving[1][:],
+                start=True,
+                stop=True,
+            )
+
+        def member(e):
+            return 0 <= e < E
+
+        def transpose_h2(e):
+            if not member(e):
+                return
+            words = h2_rows[e][:].bitcast(F32)
+            h2_t = psum.tile([P, 2, ROWS, P], F32, tag="words", bufs=2)
+            for u in range(2):
+                for c in range(ROWS):
+                    nc.tensor.transpose(h2_t[:, u, c, :], words[:, c, P * u : P * (u + 1)], identity[:])
+            h2_words[e] = h2_t
+
+        def copy_h2_words(e):
+            if not member(e):
+                return
+            grouped = work.tile([P, B, PACK], BF16, name="h2_grouped", align_bytes=64)
+            nc.scalar.copy(
+                out=grouped[:].bitcast(F32), in_=h2_words[e][:].rearrange("q u c p -> q (c p) u")
+            )
+            h2_grouped[e] = grouped
+
+        def regroup_w3(e):
+            if not member(e):
+                return
+            grouped = work.tile([P, H3, PACK], BF16, name="w3_grouped", align_bytes=64)
+            regroup(nc.vector.tensor_copy, grouped[:], w3_planes[e][:])
+            w3_grouped[e] = grouped
+
+        def regroup_heads(e):
+            if not member(e):
+                return
+            grouped = work.tile([P, 2 * S, PACK], BF16, name="heads_grouped", align_bytes=64)
+            regroup(nc.scalar.copy, grouped[:], heads_planes[e][:])
+            heads_grouped[e] = grouped
+
+        def quantise_h2(e):
+            if member(e):
+                h2_mx[e] = quantise(h2_grouped[e], B, "h2")
+
+        def quantise_w3(e):
+            if member(e):
+                w3_mx[e] = quantise(w3_grouped[e], H3, "w3")
+
+        def quantise_heads(e):
+            if member(e):
+                heads_mx[e] = quantise(heads_grouped[e], 2 * S, "heads")
+
+        def quantise_h(e):
+            if member(e):
+                h_mx[e] = quantise(h_grouped[e], B, "h")
+
+        def hidden_matmuls(e):
+            if not member(e):
+                return
+            hidden_sums[e] = []
+            for half in range(2):
+                sums = psum.tile([P, 2, B], F32, tag="hidden", bufs=3)
+                for j in range(2):
+                    t = 2 * half + j
+                    multiply(sums[:, j, :], w3_mx[e], slice(P * t, P * (t + 1)), h2_mx[e])
+                hidden_sums[e].append(sums)
+
+        def swish_and_regroup(e):
+            if not member(e):
+                return
+            h_planes = work.tile([P, PACK, B], BF16)
+            for t in range(PACK):
+                nc.scalar.activation(
+                    out=h_planes[:, t, :],
+                    in_=hidden_sums[e][t // 2][:, t % 2, :],
+                    func=ACT.Silu,
+                    bias=columns[:, ROW_B3 + PACK * e + t : ROW_B3 + PACK * e + t + 1],
+                    scale=1.0,
+                )
+            grouped = work.tile([P, B, PACK], BF16, name="h_grouped", align_bytes=64)
+            regroup(nc.vector.tensor_copy, grouped[:], h_planes[:])
+            h_grouped[e] = grouped
+
+        def head_matmuls(e):
+            if not member(e):
+                return
+            mu_sums = psum.tile([P, B], F32, tag="mu")
+            multiply(mu_sums[:], heads_mx[e], slice(0, S), h_mx[e])
+            p_sums = psum.tile([P, B], F32, tag="p")
+            multiply(p_sums[:], heads_mx[e], slice(S, 2 * S), h_mx[e])
+            head_sums[e] = (mu_sums, p_sums)
+
+        def finish(e):
+            if not member(e):
+                return
+            mu_sums, p_sums = head_sums[e]
+            tanh = work.tile([P, B], F32)
+            nc.scalar.activation(
+                out=tanh[:], in_=p_sums[:], func=ACT.Tanh, bias=tanh_bias[:, e : e + 1], scale=0.5
+            )
+            both = work.tile([P, 2, B], F32)
+            nc.vector.scalar_tensor_tensor(
+                out=both[:, 0, :],
+                in0=mu_sums[:],
+                scalar=columns[:, ROW_BMU + e : ROW_BMU + e + 1],
+                in1=state_t,
+                op0=ALU.add,
+                op1=ALU.add,
+            )
+            nc.vector.tensor_scalar(
+                out=both[:, 1, :],
+                in0=tanh[:],
+                scalar1=sigma_affine[:, 0:1],
+                scalar2=sigma_affine[:, 1:2],
+                op0=ALU.mult,
+                op1=ALU.add,
+            )
+            turned[e] = both
+
+        def transpose_back(e):
+            if not member(e):
+                return
+            back = psum.tile([P, 2, ROWS, S], F32, tag="back")
+            for o in range(2):
+                for c in range(ROWS):
+                    nc.tensor.transpose(back[:, o, c, :], turned[e][:, o, P * c : P * (c + 1)], identity[:])
+            turned_back[e] = back
+
+        def store(e):
+            if not member(e):
+                return
+            result = results.tile([P, 2, ROWS, S], F32)
+            nc.scalar.copy(out=result[:], in_=turned_back[e][:])
+            nc.sync.dma_start(out=out_0[e].rearrange("(p c) s -> p c s", c=ROWS), in_=result[:, 0])
+            nc.sync.dma_start(out=out_1[e].rearrange("(p c) s -> p c s", c=ROWS), in_=result[:, 1])
+
+        transpose_h2(0)
+        small_f32 = const.tile([P, P], F32)
+        nc.vector.tensor_copy(out=small_f32[:], in_=small_rows[:])
+        state_f32 = const.tile([P, ROWS, S], F32)
+        nc.vector.tensor_copy(out=state_f32[:], in_=state_rows[:])
+        spread = psum.tile([P, 1 + ROWS, P], F32, tag="words", bufs=2)
+        nc.tensor.transpose(spread[:, 0, :], small_f32[:], identity[:])
+        for c in range(ROWS):
+            nc.tensor.transpose(spread[:, 1 + c, :], state_f32[:, c, :], identity[:])
+        columns_and_state = const.tile([P, 1 + ROWS, P], F32)
+        nc.vector.tensor_copy(out=columns_and_state[:], in_=spread[:])
+        columns = columns_and_state[:, 0, :]
+        state_t = columns_and_state[:, 1:, :].rearrange("s c p -> s (c p)")
+
+        copy_h2_words(0)
+        exp_bounds = const.tile([P, 2], F32)
+        nc.scalar.activation(out=exp_bounds[:], in_=columns[:, ROW_MAX : ROW_MIN + 1], func=ACT.Exp)
+        table_change = const.tile([P, 1], F32)
+        nc.scalar.activation(out=table_change[:], in_=exp_bounds[:, 0:1], func=ACT.Tanh)
+
+        regroup_w3(0)
+        transpose_h2(1)
+        quantise_h2(0)
+        quantise_w3(0)
+        hidden_matmuls(0)
+
+        tanh_bias = const.tile([P, E], F32)
+        nc.vector.tensor_scalar(
+            out=tanh_bias[:],
+            in0=columns[:, ROW_BSIG:ROW_MAX],
+            scalar1=columns[:, ROW_MAX : ROW_MAX + 1],
+            scalar2=0.5,
+            op0=ALU.subtract,
+            op1=ALU.mult,
+        )
+        sigma_affine = const.tile([P, 2], F32)
+        nc.vector.tensor_scalar(
+            out=sigma_affine[:, 0:1], in0=exp_bounds[:, 0:1], scalar1=0.5, scalar2=None, op0=ALU.mult
+        )
+        nc.vector.tensor_add(out=sigma_affine[:, 1:2], in0=sigma_affine[:, 0:1], in1=exp_bounds[:, 1:2])
+
+        for i in range(E + 1):
+            head_matmuls(i - 1)
+            copy_h2_words(i + 1)
+            regroup_w3(i + 1)
+            finish(i - 1)
+            transpose_back(i - 1)
+            transpose_h2(i + 2)
+            quantise_h2(i + 1)
+            swish_and_regroup(i)
+            regroup_heads(i)
+            quantise_w3(i + 1)
+            quantise_heads(i)
+            quantise_h(i)
+            hidden_matmuls(i + 1)
+            store(i - 1)

@@ -1,3 +1,4 @@
+import math
 from contextlib import ExitStack
 
 import concourse.mybir as mybir
@@ -47,35 +48,45 @@ def tile_ensembledynamicmodel_pa_kernel(
         work = ctx.enter_context(tc.tile_pool(name="work", bufs=3))
         results = ctx.enter_context(tc.tile_pool(name="results", bufs=E))
         psum = ctx.enter_context(tc.psum_pool(name="psum", bufs=1))
+        ctx.enter_context(tc.manual_schedule())
         small_rows = const.tile([P, P], BF16)
         nc.vector.memset(small_rows[:], 0.0)
+        warm = const.tile([P, 1], F32)
+        nc.vector.memset(warm[:], 0.0)
         nc.scalar.dma_start(
             out=small_rows[ROW_B3:ROW_BMU, :], in_=b3.rearrange("e (t p) -> (e t) p", p=P)
         )
-        nc.scalar.dma_start(out=small_rows[ROW_BMU:ROW_BSIG, :], in_=bmu)
-        nc.scalar.dma_start(out=small_rows[ROW_BSIG:ROW_MAX, :], in_=bsig)
         nc.scalar.dma_start(
             out=small_rows[ROW_MAX:ROW_MIN, :], in_=max_logstd.rearrange("(o s) -> o s", o=1)
         )
         nc.scalar.dma_start(
             out=small_rows[ROW_MIN : ROW_MIN + 1, :], in_=min_logstd.rearrange("(o s) -> o s", o=1)
         )
-        state_rows = const.tile([P, ROWS, S], BF16)
-        nc.scalar.dma_start(out=state_rows[:], in_=state.rearrange("(p c) s -> p c s", c=ROWS))
+        nc.scalar.dma_start(out=small_rows[ROW_BMU:ROW_BSIG, :], in_=bmu)
+        nc.scalar.dma_start(out=small_rows[ROW_BSIG:ROW_MAX, :], in_=bsig)
+        warm_out = const.tile([P, 1], F32)
+        nc.scalar.activation(out=warm_out[:], in_=warm[:], func=ACT.Silu)
 
         h2_rows = {}
         w3_planes = {}
         heads_planes = {}
-        for e in range(E):
+
+        def load_h2(e):
+            if not 0 <= e < E:
+                return
             h2_in = inputs.tile([P, ROWS, H2], BF16, name="h2_rows%d" % e)
             nc.sync.dma_start(out=h2_in[:], in_=h2[e].rearrange("(p c) k -> p c k", c=ROWS))
             h2_rows[e] = h2_in
+
+        def load_w3(e):
             w3_in = inputs.tile([P, PACK, H3], BF16, name="w3_planes%d" % e)
             nc.sync.dma_start(
                 out=w3_in[:].rearrange("q (u r) n -> q u (r n)", u=2),
                 in_=W3[e].rearrange("(u q r) n -> q u (r n)", u=2, r=2),
             )
             w3_planes[e] = w3_in
+
+        def load_heads(e):
             heads_in = inputs.tile([P, PACK, 2 * S], BF16, name="heads_planes%d" % e)
             nc.sync.dma_start(
                 out=heads_in[:, :, 0:S], in_=Wmu[e].rearrange("(t p) s -> p t s", p=P)
@@ -85,8 +96,21 @@ def tile_ensembledynamicmodel_pa_kernel(
             )
             heads_planes[e] = heads_in
 
+        state_rows = const.tile([P, ROWS, S], BF16)
+        load_w3(0)
+        load_h2(0)
+        nc.sync.dma_start(out=state_rows[:], in_=state.rearrange("(p c) s -> p c s", c=ROWS))
+        load_h2(1)
+        load_heads(0)
+        for e in range(1, E):
+            load_w3(e)
+            load_h2(e + 1)
+            load_heads(e)
+
         identity = const.tile([P, P], F32)
         make_identity(nc, identity[:])
+        identity_bf16 = const.tile([P, P], BF16)
+        nc.gpsimd.tensor_copy(out=identity_bf16[:], in_=identity[:])
 
         h2_words = {}
         h2_grouped = {}
@@ -96,7 +120,9 @@ def tile_ensembledynamicmodel_pa_kernel(
         heads_grouped = {}
         heads_mx = {}
         hidden_sums = {}
+        h_planes = {}
         h_grouped = {}
+        tanhs = {}
         h_mx = {}
         head_sums = {}
         turned = {}
@@ -186,57 +212,70 @@ def tile_ensembledynamicmodel_pa_kernel(
                     multiply(sums[:, j, :], w3_mx[e], slice(P * t, P * (t + 1)), h2_mx[e])
                 hidden_sums[e].append(sums)
 
-        def swish_and_regroup(e):
+        def swish(e):
             if not member(e):
                 return
-            h_planes = work.tile([P, PACK, B], BF16)
+            planes = work.tile([P, PACK, B], BF16, name="h_planes")
             for t in range(PACK):
                 nc.scalar.activation(
-                    out=h_planes[:, t, :],
+                    out=planes[:, t, :],
                     in_=hidden_sums[e][t // 2][:, t % 2, :],
                     func=ACT.Silu,
                     bias=columns[:, ROW_B3 + PACK * e + t : ROW_B3 + PACK * e + t + 1],
                     scale=1.0,
                 )
+            h_planes[e] = planes
+
+        def regroup_h(e):
+            if not member(e):
+                return
             grouped = work.tile([P, B, PACK], BF16, name="h_grouped", align_bytes=64)
-            regroup(nc.vector.tensor_copy, grouped[:], h_planes[:])
+            regroup(nc.vector.tensor_copy, grouped[:], h_planes[e][:])
             h_grouped[e] = grouped
 
         def head_matmuls(e):
             if not member(e):
                 return
-            mu_sums = psum.tile([P, B], F32, tag="mu")
-            multiply(mu_sums[:], heads_mx[e], slice(0, S), h_mx[e])
             p_sums = psum.tile([P, B], F32, tag="p")
             multiply(p_sums[:], heads_mx[e], slice(S, 2 * S), h_mx[e])
+            mu_sums = psum.tile([P, B], F32, tag="mu")
+            multiply(mu_sums[:], heads_mx[e], slice(0, S), h_mx[e])
             head_sums[e] = (mu_sums, p_sums)
 
-        def finish(e):
+        def add_mu(e):
             if not member(e):
                 return
-            mu_sums, p_sums = head_sums[e]
-            tanh = work.tile([P, B], F32)
-            nc.scalar.activation(
-                out=tanh[:], in_=p_sums[:], func=ACT.Tanh, bias=tanh_bias[:, e : e + 1], scale=0.5
-            )
-            both = work.tile([P, 2, B], F32)
+            both = work.tile([P, 2, B], F32, name="both")
             nc.vector.scalar_tensor_tensor(
                 out=both[:, 0, :],
-                in0=mu_sums[:],
+                in0=head_sums[e][0][:],
                 scalar=columns[:, ROW_BMU + e : ROW_BMU + e + 1],
-                in1=state_t,
+                in1=state_t[:],
                 op0=ALU.add,
                 op1=ALU.add,
             )
+            turned[e] = both
+
+        def tanh_p(e):
+            if not member(e):
+                return
+            tanh = work.tile([P, B], F32, name="tanh")
+            nc.scalar.activation(
+                out=tanh[:], in_=head_sums[e][1][:], func=ACT.Tanh, bias=tanh_bias[:, e : e + 1], scale=0.5
+            )
+            tanhs[e] = tanh
+
+        def scale_sigma(e):
+            if not member(e):
+                return
             nc.vector.tensor_scalar(
-                out=both[:, 1, :],
-                in0=tanh[:],
+                out=turned[e][:, 1, :],
+                in0=tanhs[e][:],
                 scalar1=sigma_affine[:, 0:1],
                 scalar2=sigma_affine[:, 1:2],
                 op0=ALU.mult,
                 op1=ALU.add,
             )
-            turned[e] = both
 
         def transpose_back(e):
             if not member(e):
@@ -256,33 +295,33 @@ def tile_ensembledynamicmodel_pa_kernel(
             nc.sync.dma_start(out=out_1[e].rearrange("(p c) s -> p c s", c=ROWS), in_=result[:, 1])
 
         transpose_h2(0)
-        small_f32 = const.tile([P, P], F32)
-        nc.vector.tensor_copy(out=small_f32[:], in_=small_rows[:])
-        state_f32 = const.tile([P, ROWS, S], F32)
-        nc.vector.tensor_copy(out=state_f32[:], in_=state_rows[:])
-        spread = psum.tile([P, 1 + ROWS, P], F32, tag="words", bufs=2)
-        nc.tensor.transpose(spread[:, 0, :], small_f32[:], identity[:])
-        for c in range(ROWS):
-            nc.tensor.transpose(spread[:, 1 + c, :], state_f32[:, c, :], identity[:])
-        columns_and_state = const.tile([P, 1 + ROWS, P], F32)
-        nc.vector.tensor_copy(out=columns_and_state[:], in_=spread[:])
-        columns = columns_and_state[:, 0, :]
-        state_t = columns_and_state[:, 1:, :].rearrange("s c p -> s (c p)")
-
-        copy_h2_words(0)
-        exp_bounds = const.tile([P, 2], F32)
-        nc.scalar.activation(out=exp_bounds[:], in_=columns[:, ROW_MAX : ROW_MIN + 1], func=ACT.Exp)
-        table_change = const.tile([P, 1], F32)
-        nc.scalar.activation(out=table_change[:], in_=exp_bounds[:, 0:1], func=ACT.Tanh)
-
         regroup_w3(0)
-        transpose_h2(1)
-        quantise_h2(0)
+        copy_h2_words(0)
+        spread = psum.tile([P, 1 + ROWS, P], BF16, tag="words", bufs=2)
+        nc.tensor.transpose(spread[:, 0, :], small_rows[:], identity_bf16[:])
+        for c in range(ROWS):
+            nc.tensor.transpose(spread[:, 1 + c, :], state_rows[:, c, :], identity_bf16[:])
         quantise_w3(0)
+        quantise_h2(0)
+        columns = const.tile([P, P], F32)
+        nc.vector.tensor_copy(out=columns[:], in_=spread[:, 0, :])
+        state_t = const.tile([P, B], BF16)
+        nc.vector.tensor_copy(out=state_t[:], in_=spread[:, 1:, :].rearrange("s c p -> s (c p)"))
+        transpose_h2(1)
+        copy_h2_words(1)
         hidden_matmuls(0)
+        regroup_heads(0)
 
+        base = const.tile([P, 2], F32)
+        nc.gpsimd.tensor_scalar(
+            out=base[:], in0=columns[:, ROW_MAX : ROW_MIN + 1], scalar1=0.0, scalar2=math.e, op0=ALU.mult, op1=ALU.add
+        )
+        exp_bounds = const.tile([P, 2], F32)
+        nc.gpsimd.tensor_tensor(
+            out=exp_bounds[:], in0=base[:], in1=columns[:, ROW_MAX : ROW_MIN + 1], op=ALU.pow
+        )
         tanh_bias = const.tile([P, E], F32)
-        nc.vector.tensor_scalar(
+        nc.gpsimd.tensor_scalar(
             out=tanh_bias[:],
             in0=columns[:, ROW_BSIG:ROW_MAX],
             scalar1=columns[:, ROW_MAX : ROW_MAX + 1],
@@ -291,23 +330,39 @@ def tile_ensembledynamicmodel_pa_kernel(
             op1=ALU.mult,
         )
         sigma_affine = const.tile([P, 2], F32)
-        nc.vector.tensor_scalar(
-            out=sigma_affine[:, 0:1], in0=exp_bounds[:, 0:1], scalar1=0.5, scalar2=None, op0=ALU.mult
+        nc.gpsimd.tensor_scalar(
+            out=sigma_affine[:, 0:1], in0=exp_bounds[:, 0:1], scalar1=0.5, scalar2=0.0, op0=ALU.mult, op1=ALU.add
         )
-        nc.vector.tensor_add(out=sigma_affine[:, 1:2], in0=sigma_affine[:, 0:1], in1=exp_bounds[:, 1:2])
+        nc.gpsimd.tensor_tensor(
+            out=sigma_affine[:, 1:2], in0=sigma_affine[:, 0:1], in1=exp_bounds[:, 1:2], op=ALU.add
+        )
 
-        for i in range(E + 1):
-            head_matmuls(i - 1)
-            copy_h2_words(i + 1)
-            regroup_w3(i + 1)
-            finish(i - 1)
-            transpose_back(i - 1)
-            transpose_h2(i + 2)
-            quantise_h2(i + 1)
-            swish_and_regroup(i)
-            regroup_heads(i)
-            quantise_w3(i + 1)
-            quantise_heads(i)
-            quantise_h(i)
-            hidden_matmuls(i + 1)
-            store(i - 1)
+        regroup_w3(1)
+        quantise_h2(1)
+        transpose_h2(2)
+        swish(0)
+        copy_h2_words(2)
+        quantise_heads(0)
+        quantise_w3(1)
+        regroup_heads(1)
+        hidden_matmuls(1)
+        quantise_h2(2)
+
+        for r in range(E + 2):
+            transpose_h2(r + 3)
+            regroup_h(r)
+            add_mu(r - 1)
+            scale_sigma(r - 1)
+            swish(r + 1)
+            transpose_back(r - 1)
+            regroup_w3(r + 2)
+            copy_h2_words(r + 3)
+            quantise_h(r)
+            head_matmuls(r)
+            quantise_w3(r + 2)
+            hidden_matmuls(r + 2)
+            quantise_h2(r + 3)
+            store(r - 1)
+            regroup_heads(r + 2)
+            quantise_heads(r + 1)
+            tanh_p(r)

@@ -22,8 +22,7 @@ H3 = 512
 S = 128
 RUN = 4
 
-ROW_B3 = 0
-ROW_BMU = ROW_B3 + E * PACK
+ROW_BMU = 0
 ROW_BSIG = ROW_BMU + E
 ROW_MAX = ROW_BSIG + E
 ROW_MIN = ROW_MAX + 1
@@ -49,23 +48,19 @@ def tile_ensembledynamicmodel_pa_kernel(
         results = ctx.enter_context(tc.tile_pool(name="results", bufs=E))
         psum = ctx.enter_context(tc.psum_pool(name="psum", bufs=1))
         ctx.enter_context(tc.manual_schedule())
+        b3_rows = const.tile([P, P], BF16)
+        nc.vector.memset(b3_rows[:], 0.0)
         small_rows = const.tile([P, P], BF16)
         nc.vector.memset(small_rows[:], 0.0)
         warm = const.tile([P, 1], F32)
         nc.vector.memset(warm[:], 0.0)
-        nc.scalar.dma_start(
-            out=small_rows[ROW_B3:ROW_BMU, :], in_=b3.rearrange("e (t p) -> (e t) p", p=P)
-        )
-        nc.scalar.dma_start(
-            out=small_rows[ROW_MAX:ROW_MIN, :], in_=max_logstd.rearrange("(o s) -> o s", o=1)
-        )
-        nc.scalar.dma_start(
-            out=small_rows[ROW_MIN : ROW_MIN + 1, :], in_=min_logstd.rearrange("(o s) -> o s", o=1)
-        )
-        nc.scalar.dma_start(out=small_rows[ROW_BMU:ROW_BSIG, :], in_=bmu)
-        nc.scalar.dma_start(out=small_rows[ROW_BSIG:ROW_MAX, :], in_=bsig)
         warm_out = const.tile([P, 1], F32)
         nc.scalar.activation(out=warm_out[:], in_=warm[:], func=ACT.Silu)
+
+        identity = const.tile([P, P], F32)
+        make_identity(nc, identity[:])
+        identity_bf16 = const.tile([P, P], BF16)
+        nc.vector.tensor_copy(out=identity_bf16[:], in_=identity[:])
 
         h2_rows = {}
         w3_planes = {}
@@ -99,18 +94,25 @@ def tile_ensembledynamicmodel_pa_kernel(
         state_rows = const.tile([P, ROWS, S], BF16)
         load_w3(0)
         load_h2(0)
-        nc.sync.dma_start(out=state_rows[:], in_=state.rearrange("(p c) s -> p c s", c=ROWS))
+        nc.sync.dma_start(out=b3_rows[0 : E * PACK, :], in_=b3.rearrange("e (t p) -> (e t) p", p=P))
+        nc.sync.dma_start(
+            out=small_rows[ROW_MAX:ROW_MIN, :], in_=max_logstd.rearrange("(o s) -> o s", o=1)
+        )
+        nc.sync.dma_start(
+            out=small_rows[ROW_MIN : ROW_MIN + 1, :], in_=min_logstd.rearrange("(o s) -> o s", o=1)
+        )
         load_h2(1)
+        load_w3(1)
+        nc.sync.dma_start(out=small_rows[ROW_BMU:ROW_BSIG, :], in_=bmu)
+        nc.sync.dma_start(out=small_rows[ROW_BSIG:ROW_MAX, :], in_=bsig)
         load_heads(0)
-        for e in range(1, E):
+        nc.sync.dma_start(out=state_rows[:], in_=state.rearrange("(p c) s -> p c s", c=ROWS))
+        load_h2(2)
+        for e in range(2, E):
             load_w3(e)
+            load_heads(e - 1)
             load_h2(e + 1)
-            load_heads(e)
-
-        identity = const.tile([P, P], F32)
-        make_identity(nc, identity[:])
-        identity_bf16 = const.tile([P, P], BF16)
-        nc.gpsimd.tensor_copy(out=identity_bf16[:], in_=identity[:])
+        load_heads(E - 1)
 
         h2_words = {}
         h2_grouped = {}
@@ -182,7 +184,8 @@ def tile_ensembledynamicmodel_pa_kernel(
             if not member(e):
                 return
             grouped = work.tile([P, 2 * S, PACK], BF16, name="heads_grouped", align_bytes=64)
-            regroup(nc.scalar.copy, grouped[:], heads_planes[e][:])
+            copy = nc.scalar.copy if e < E - 1 else nc.vector.tensor_copy
+            regroup(copy, grouped[:], heads_planes[e][:])
             heads_grouped[e] = grouped
 
         def quantise_h2(e):
@@ -221,7 +224,7 @@ def tile_ensembledynamicmodel_pa_kernel(
                     out=planes[:, t, :],
                     in_=hidden_sums[e][t // 2][:, t % 2, :],
                     func=ACT.Silu,
-                    bias=columns[:, ROW_B3 + PACK * e + t : ROW_B3 + PACK * e + t + 1],
+                    bias=b3_columns[:, PACK * e + t : PACK * e + t + 1],
                     scale=1.0,
                 )
             h_planes[e] = planes
@@ -277,41 +280,57 @@ def tile_ensembledynamicmodel_pa_kernel(
                 op1=ALU.add,
             )
 
-        def transpose_back(e):
+        def transpose_back(e, o, back):
+            for c in range(ROWS):
+                nc.tensor.transpose(back[:, c, :], turned[e][:, o, P * c : P * (c + 1)], identity[:])
+
+        def transpose_both_back(e):
             if not member(e):
                 return
             back = psum.tile([P, 2, ROWS, S], F32, tag="back")
             for o in range(2):
-                for c in range(ROWS):
-                    nc.tensor.transpose(back[:, o, c, :], turned[e][:, o, P * c : P * (c + 1)], identity[:])
+                transpose_back(e, o, back[:, o])
             turned_back[e] = back
 
         def store(e):
             if not member(e):
                 return
             result = results.tile([P, 2, ROWS, S], F32)
-            nc.scalar.copy(out=result[:], in_=turned_back[e][:])
+            copy = nc.scalar.copy if e < E - 2 else nc.vector.tensor_copy
+            copy(out=result[:], in_=turned_back[e][:])
             nc.sync.dma_start(out=out_0[e].rearrange("(p c) s -> p c s", c=ROWS), in_=result[:, 0])
             nc.sync.dma_start(out=out_1[e].rearrange("(p c) s -> p c s", c=ROWS), in_=result[:, 1])
 
         transpose_h2(0)
         regroup_w3(0)
         copy_h2_words(0)
-        spread = psum.tile([P, 1 + ROWS, P], BF16, tag="words", bufs=2)
+        b3_spread = psum.tile([P, P], BF16, tag="back")
+        nc.tensor.transpose(b3_spread[:], b3_rows[:], identity_bf16[:])
+        transpose_h2(1)
+        quantise_w3(0)
+        quantise_h2(0)
+        b3_columns = const.tile([P, P], F32)
+        nc.vector.tensor_copy(out=b3_columns[:], in_=b3_spread[:])
+        copy_h2_words(1)
+        hidden_matmuls(0)
+
+        transpose_h2(2)
+        regroup_w3(1)
+        swish(0)
+        quantise_h2(1)
+        quantise_w3(1)
+        regroup_heads(0)
+        copy_h2_words(2)
+        spread = psum.tile([P, 1 + ROWS, P], BF16, tag="p")
         nc.tensor.transpose(spread[:, 0, :], small_rows[:], identity_bf16[:])
         for c in range(ROWS):
             nc.tensor.transpose(spread[:, 1 + c, :], state_rows[:, c, :], identity_bf16[:])
-        quantise_w3(0)
-        quantise_h2(0)
+        hidden_matmuls(1)
+        regroup_h(0)
         columns = const.tile([P, P], F32)
         nc.vector.tensor_copy(out=columns[:], in_=spread[:, 0, :])
         state_t = const.tile([P, B], BF16)
         nc.vector.tensor_copy(out=state_t[:], in_=spread[:, 1:, :].rearrange("s c p -> s (c p)"))
-        transpose_h2(1)
-        copy_h2_words(1)
-        hidden_matmuls(0)
-        regroup_heads(0)
-
         base = const.tile([P, 2], F32)
         nc.gpsimd.tensor_scalar(
             out=base[:], in0=columns[:, ROW_MAX : ROW_MIN + 1], scalar1=0.0, scalar2=math.e, op0=ALU.mult, op1=ALU.add
@@ -337,32 +356,36 @@ def tile_ensembledynamicmodel_pa_kernel(
             out=sigma_affine[:, 1:2], in0=sigma_affine[:, 0:1], in1=exp_bounds[:, 1:2], op=ALU.add
         )
 
-        regroup_w3(1)
-        quantise_h2(1)
-        transpose_h2(2)
-        swish(0)
-        copy_h2_words(2)
-        quantise_heads(0)
-        quantise_w3(1)
-        regroup_heads(1)
-        hidden_matmuls(1)
-        quantise_h2(2)
-
-        for r in range(E + 2):
+        for r in range(E):
             transpose_h2(r + 3)
-            regroup_h(r)
+            if r:
+                regroup_h(r)
             add_mu(r - 1)
             scale_sigma(r - 1)
             swish(r + 1)
-            transpose_back(r - 1)
+            transpose_both_back(r - 1)
             regroup_w3(r + 2)
-            copy_h2_words(r + 3)
             quantise_h(r)
+            quantise_heads(r)
+            regroup_heads(r + 1)
+            copy_h2_words(r + 3)
             head_matmuls(r)
+            quantise_h2(r + 2)
             quantise_w3(r + 2)
             hidden_matmuls(r + 2)
-            quantise_h2(r + 3)
             store(r - 1)
-            regroup_heads(r + 2)
-            quantise_heads(r + 1)
             tanh_p(r)
+
+        e = E - 1
+        add_mu(e)
+        mu_back = psum.tile([P, ROWS, S], F32, tag="back")
+        transpose_back(e, 0, mu_back)
+        scale_sigma(e)
+        mu_result = results.tile([P, ROWS, S], F32, name="mu_result")
+        nc.vector.tensor_copy(out=mu_result[:], in_=mu_back[:])
+        nc.sync.dma_start(out=out_0[e].rearrange("(p c) s -> p c s", c=ROWS), in_=mu_result[:])
+        sigma_back = psum.tile([P, ROWS, S], F32, tag="mu")
+        transpose_back(e, 1, sigma_back)
+        sigma_result = results.tile([P, ROWS, S], F32, name="sigma_result")
+        nc.scalar.copy(out=sigma_result[:], in_=sigma_back[:])
+        nc.sync.dma_start(out=out_1[e].rearrange("(p c) s -> p c s", c=ROWS), in_=sigma_result[:])

@@ -92,8 +92,8 @@ def tile_ensembledynamicmodel_pa_kernel(
             heads_planes[e] = heads_in
 
         state_rows = const.tile([P, ROWS, S], BF16)
-        load_w3(0)
         load_h2(0)
+        load_w3(0)
         nc.sync.dma_start(out=b3_rows[0 : E * PACK, :], in_=b3.rearrange("e (t p) -> (e t) p", p=P))
         nc.sync.dma_start(
             out=small_rows[ROW_MAX:ROW_MIN, :], in_=max_logstd.rearrange("(o s) -> o s", o=1)
@@ -302,13 +302,13 @@ def tile_ensembledynamicmodel_pa_kernel(
             nc.sync.dma_start(out=out_1[e].rearrange("(p c) s -> p c s", c=ROWS), in_=result[:, 1])
 
         transpose_h2(0)
-        regroup_w3(0)
         copy_h2_words(0)
+        regroup_w3(0)
         b3_spread = psum.tile([P, P], BF16, tag="back")
         nc.tensor.transpose(b3_spread[:], b3_rows[:], identity_bf16[:])
         transpose_h2(1)
-        quantise_w3(0)
         quantise_h2(0)
+        quantise_w3(0)
         b3_columns = const.tile([P, P], F32)
         nc.vector.tensor_copy(out=b3_columns[:], in_=b3_spread[:])
         copy_h2_words(1)
@@ -316,65 +316,65 @@ def tile_ensembledynamicmodel_pa_kernel(
 
         transpose_h2(2)
         regroup_w3(1)
-        swish(0)
-        quantise_h2(1)
-        quantise_w3(1)
         regroup_heads(0)
+        swish(0)
         copy_h2_words(2)
         spread = psum.tile([P, 1 + ROWS, P], BF16, tag="p")
         nc.tensor.transpose(spread[:, 0, :], small_rows[:], identity_bf16[:])
         for c in range(ROWS):
             nc.tensor.transpose(spread[:, 1 + c, :], state_rows[:, c, :], identity_bf16[:])
+        quantise_h2(1)
+        quantise_w3(1)
         hidden_matmuls(1)
-        regroup_h(0)
-        columns = const.tile([P, P], F32)
-        nc.vector.tensor_copy(out=columns[:], in_=spread[:, 0, :])
-        state_t = const.tile([P, B], BF16)
-        nc.vector.tensor_copy(out=state_t[:], in_=spread[:, 1:, :].rearrange("s c p -> s (c p)"))
-        base = const.tile([P, 2], F32)
-        nc.gpsimd.tensor_scalar(
-            out=base[:], in0=columns[:, ROW_MAX : ROW_MIN + 1], scalar1=0.0, scalar2=math.e, op0=ALU.mult, op1=ALU.add
-        )
-        exp_bounds = const.tile([P, 2], F32)
-        nc.gpsimd.tensor_tensor(
-            out=exp_bounds[:], in0=base[:], in1=columns[:, ROW_MAX : ROW_MIN + 1], op=ALU.pow
-        )
-        tanh_bias = const.tile([P, E], F32)
-        nc.gpsimd.tensor_scalar(
-            out=tanh_bias[:],
-            in0=columns[:, ROW_BSIG:ROW_MAX],
-            scalar1=columns[:, ROW_MAX : ROW_MAX + 1],
-            scalar2=0.5,
-            op0=ALU.subtract,
-            op1=ALU.mult,
-        )
-        sigma_affine = const.tile([P, 2], F32)
-        nc.gpsimd.tensor_scalar(
-            out=sigma_affine[:, 0:1], in0=exp_bounds[:, 0:1], scalar1=0.5, scalar2=0.0, op0=ALU.mult, op1=ALU.add
-        )
-        nc.gpsimd.tensor_tensor(
-            out=sigma_affine[:, 1:2], in0=sigma_affine[:, 0:1], in1=exp_bounds[:, 1:2], op=ALU.add
-        )
+        quantise_heads(0)
 
         for r in range(E):
             transpose_h2(r + 3)
-            if r:
-                regroup_h(r)
+            regroup_w3(r + 2)
+            if r == 0:
+                columns = const.tile([P, P], F32)
+                nc.vector.tensor_copy(out=columns[:], in_=spread[:, 0, :])
+                state_t = const.tile([P, B], BF16)
+                nc.vector.tensor_copy(out=state_t[:], in_=spread[:, 1:, :].rearrange("s c p -> s (c p)"))
+                base = const.tile([P, 2], F32)
+                nc.gpsimd.tensor_scalar(
+                    out=base[:], in0=columns[:, ROW_MAX : ROW_MIN + 1], scalar1=0.0, scalar2=math.e, op0=ALU.mult, op1=ALU.add
+                )
+                exp_bounds = const.tile([P, 2], F32)
+                nc.gpsimd.tensor_tensor(
+                    out=exp_bounds[:], in0=base[:], in1=columns[:, ROW_MAX : ROW_MIN + 1], op=ALU.pow
+                )
+                tanh_bias = const.tile([P, E], F32)
+                nc.gpsimd.tensor_scalar(
+                    out=tanh_bias[:],
+                    in0=columns[:, ROW_BSIG:ROW_MAX],
+                    scalar1=columns[:, ROW_MAX : ROW_MAX + 1],
+                    scalar2=0.5,
+                    op0=ALU.subtract,
+                    op1=ALU.mult,
+                )
+                sigma_affine = const.tile([P, 2], F32)
+                nc.gpsimd.tensor_scalar(
+                    out=sigma_affine[:, 0:1], in0=exp_bounds[:, 0:1], scalar1=0.5, scalar2=0.0, op0=ALU.mult, op1=ALU.add
+                )
+                nc.gpsimd.tensor_tensor(
+                    out=sigma_affine[:, 1:2], in0=sigma_affine[:, 0:1], in1=exp_bounds[:, 1:2], op=ALU.add
+                )
+            regroup_h(r)
             add_mu(r - 1)
             scale_sigma(r - 1)
-            swish(r + 1)
             transpose_both_back(r - 1)
-            regroup_w3(r + 2)
-            quantise_h(r)
-            quantise_heads(r)
             regroup_heads(r + 1)
+            swish(r + 1)
             copy_h2_words(r + 3)
-            head_matmuls(r)
             quantise_h2(r + 2)
+            quantise_h(r)
+            head_matmuls(r)
             quantise_w3(r + 2)
             hidden_matmuls(r + 2)
-            store(r - 1)
+            quantise_heads(r + 1)
             tanh_p(r)
+            store(r - 1)
 
         e = E - 1
         add_mu(e)

@@ -45,7 +45,7 @@ def tile_ensembledynamicmodel_pa_kernel(
         const = ctx.enter_context(tc.tile_pool(name="const", bufs=1))
         inputs = ctx.enter_context(tc.tile_pool(name="inputs", bufs=1))
         work = ctx.enter_context(tc.tile_pool(name="work", bufs=3))
-        results = ctx.enter_context(tc.tile_pool(name="results", bufs=E))
+        results = ctx.enter_context(tc.tile_pool(name="results", bufs=E + 1))
         psum = ctx.enter_context(tc.psum_pool(name="psum", bufs=1))
         ctx.enter_context(tc.manual_schedule())
         b3_rows = const.tile([P, P], BF16)
@@ -154,6 +154,9 @@ def tile_ensembledynamicmodel_pa_kernel(
         def member(e):
             return 0 <= e < E
 
+        whole = slice(0, B)
+        halves = [slice(0, P), slice(P, B)]
+
         def transpose_h2(e):
             if not member(e):
                 return
@@ -200,10 +203,6 @@ def tile_ensembledynamicmodel_pa_kernel(
             if member(e):
                 heads_mx[e] = quantise(heads_grouped[e], 2 * S, "heads")
 
-        def quantise_h(e):
-            if member(e):
-                h_mx[e] = quantise(h_grouped[e], B, "h")
-
         def hidden_matmuls(e):
             if not member(e):
                 return
@@ -215,91 +214,104 @@ def tile_ensembledynamicmodel_pa_kernel(
                     multiply(sums[:, j, :], w3_mx[e], slice(P * t, P * (t + 1)), h2_mx[e])
                 hidden_sums[e].append(sums)
 
-        def swish(e):
+        def swish(e, cols):
             if not member(e):
                 return
-            planes = work.tile([P, PACK, B], BF16, name="h_planes")
+            width = cols.stop - cols.start
+            planes = work.tile([P, PACK, width], BF16, name="h_planes")
             for t in range(PACK):
                 nc.scalar.activation(
                     out=planes[:, t, :],
-                    in_=hidden_sums[e][t // 2][:, t % 2, :],
+                    in_=hidden_sums[e][t // 2][:, t % 2, cols],
                     func=ACT.Silu,
                     bias=b3_columns[:, PACK * e + t : PACK * e + t + 1],
                     scale=1.0,
                 )
-            h_planes[e] = planes
+            h_planes[e, cols.start] = planes
 
-        def regroup_h(e):
+        def regroup_h(e, cols):
             if not member(e):
                 return
-            grouped = work.tile([P, B, PACK], BF16, name="h_grouped", align_bytes=64)
-            regroup(nc.vector.tensor_copy, grouped[:], h_planes[e][:])
-            h_grouped[e] = grouped
+            width = cols.stop - cols.start
+            grouped = work.tile([P, width, PACK], BF16, name="h_grouped", align_bytes=64)
+            regroup(nc.vector.tensor_copy, grouped[:], h_planes[e, cols.start][:])
+            h_grouped[e, cols.start] = grouped
 
-        def head_matmuls(e):
+        def quantise_h(e, cols):
+            if member(e):
+                h_mx[e, cols.start] = quantise(h_grouped[e, cols.start], cols.stop - cols.start, "h")
+
+        def head_matmuls(e, cols, p_tag="p", mu_tag="mu"):
             if not member(e):
                 return
-            p_sums = psum.tile([P, B], F32, tag="p")
-            multiply(p_sums[:], heads_mx[e], slice(S, 2 * S), h_mx[e])
-            mu_sums = psum.tile([P, B], F32, tag="mu")
-            multiply(mu_sums[:], heads_mx[e], slice(0, S), h_mx[e])
-            head_sums[e] = (mu_sums, p_sums)
+            width = cols.stop - cols.start
+            p_sums = psum.tile([P, width], F32, tag=p_tag, bufs=2 if p_tag == "words" else 1)
+            multiply(p_sums[:], heads_mx[e], slice(S, 2 * S), h_mx[e, cols.start])
+            mu_sums = psum.tile([P, width], F32, tag=mu_tag, bufs=3 if mu_tag == "hidden" else 1)
+            multiply(mu_sums[:], heads_mx[e], slice(0, S), h_mx[e, cols.start])
+            head_sums[e, cols.start] = (mu_sums, p_sums)
 
-        def add_mu(e):
+        def add_mu(e, cols):
             if not member(e):
                 return
-            both = work.tile([P, 2, B], F32, name="both")
+            both = work.tile([P, 2, cols.stop - cols.start], F32, name="both")
             nc.vector.scalar_tensor_tensor(
                 out=both[:, 0, :],
-                in0=head_sums[e][0][:],
+                in0=head_sums[e, cols.start][0][:],
                 scalar=columns[:, ROW_BMU + e : ROW_BMU + e + 1],
-                in1=state_t[:],
+                in1=state_t[:, cols],
                 op0=ALU.add,
                 op1=ALU.add,
             )
-            turned[e] = both
+            turned[e, cols.start] = both
 
-        def tanh_p(e):
+        def tanh_p(e, cols):
             if not member(e):
                 return
-            tanh = work.tile([P, B], F32, name="tanh")
+            tanh = work.tile([P, cols.stop - cols.start], F32, name="tanh")
             nc.scalar.activation(
-                out=tanh[:], in_=head_sums[e][1][:], func=ACT.Tanh, bias=tanh_bias[:, e : e + 1], scale=0.5
+                out=tanh[:],
+                in_=head_sums[e, cols.start][1][:],
+                func=ACT.Tanh,
+                bias=tanh_bias[:, e : e + 1],
+                scale=0.5,
             )
-            tanhs[e] = tanh
+            tanhs[e, cols.start] = tanh
 
-        def scale_sigma(e):
+        def scale_sigma(e, cols):
             if not member(e):
                 return
             nc.vector.tensor_scalar(
-                out=turned[e][:, 1, :],
-                in0=tanhs[e][:],
+                out=turned[e, cols.start][:, 1, :],
+                in0=tanhs[e, cols.start][:],
                 scalar1=sigma_affine[:, 0:1],
                 scalar2=sigma_affine[:, 1:2],
                 op0=ALU.mult,
                 op1=ALU.add,
             )
 
-        def transpose_back(e, o, back):
-            for c in range(ROWS):
-                nc.tensor.transpose(back[:, c, :], turned[e][:, o, P * c : P * (c + 1)], identity[:])
-
-        def transpose_both_back(e):
+        def transpose_back(e, cols, tag="back"):
             if not member(e):
                 return
-            back = psum.tile([P, 2, ROWS, S], F32, tag="back")
+            rows = (cols.stop - cols.start) // P
+            back = psum.tile([P, 2, rows, S], F32, tag=tag)
             for o in range(2):
-                transpose_back(e, o, back[:, o])
-            turned_back[e] = back
+                for c in range(rows):
+                    nc.tensor.transpose(
+                        back[:, o, c, :], turned[e, cols.start][:, o, P * c : P * (c + 1)], identity[:]
+                    )
+            turned_back[e, cols.start] = back
 
-        def store(e):
+        def store(e, cols, copy):
             if not member(e):
                 return
-            result = results.tile([P, 2, ROWS, S], F32)
-            copy = nc.scalar.copy if e < E - 2 else nc.vector.tensor_copy
-            copy(out=result[:], in_=turned_back[e][:])
-            nc.sync.dma_start(out=out_0[e].rearrange("(p c) s -> p c s", c=ROWS), in_=result[:, 0])
-            nc.sync.dma_start(out=out_1[e].rearrange("(p c) s -> p c s", c=ROWS), in_=result[:, 1])
+            rows = slice(cols.start // P, cols.stop // P)
+            result = results.tile([P, 2, rows.stop - rows.start, S], F32)
+            copy(out=result[:], in_=turned_back[e, cols.start][:])
+            for o, out in enumerate((out_0, out_1)):
+                nc.sync.dma_start(
+                    out=out[e].rearrange("(p c) s -> p c s", c=ROWS)[:, rows, :], in_=result[:, o]
+                )
 
         transpose_h2(0)
         copy_h2_words(0)
@@ -317,7 +329,7 @@ def tile_ensembledynamicmodel_pa_kernel(
         transpose_h2(2)
         regroup_w3(1)
         regroup_heads(0)
-        swish(0)
+        swish(0, whole)
         copy_h2_words(2)
         spread = psum.tile([P, 1 + ROWS, P], BF16, tag="p")
         nc.tensor.transpose(spread[:, 0, :], small_rows[:], identity_bf16[:])
@@ -328,7 +340,7 @@ def tile_ensembledynamicmodel_pa_kernel(
         hidden_matmuls(1)
         quantise_heads(0)
 
-        for r in range(E):
+        for r in range(E - 1):
             transpose_h2(r + 3)
             regroup_w3(r + 2)
             if r == 0:
@@ -360,32 +372,42 @@ def tile_ensembledynamicmodel_pa_kernel(
                 nc.gpsimd.tensor_tensor(
                     out=sigma_affine[:, 1:2], in0=sigma_affine[:, 0:1], in1=exp_bounds[:, 1:2], op=ALU.add
                 )
-            regroup_h(r)
-            add_mu(r - 1)
-            scale_sigma(r - 1)
-            transpose_both_back(r - 1)
+            regroup_h(r, whole)
+            add_mu(r - 1, whole)
+            scale_sigma(r - 1, whole)
+            transpose_back(r - 1, whole)
             regroup_heads(r + 1)
-            swish(r + 1)
+            for cols in [whole] if r + 1 < E - 1 else halves:
+                swish(r + 1, cols)
             copy_h2_words(r + 3)
             quantise_h2(r + 2)
-            quantise_h(r)
-            head_matmuls(r)
+            quantise_h(r, whole)
+            head_matmuls(r, whole)
             quantise_w3(r + 2)
             hidden_matmuls(r + 2)
             quantise_heads(r + 1)
-            tanh_p(r)
-            store(r - 1)
+            tanh_p(r, whole)
+            store(r - 1, whole, nc.scalar.copy)
 
-        e = E - 1
-        add_mu(e)
-        mu_back = psum.tile([P, ROWS, S], F32, tag="back")
-        transpose_back(e, 0, mu_back)
-        scale_sigma(e)
-        mu_result = results.tile([P, ROWS, S], F32, name="mu_result")
-        nc.vector.tensor_copy(out=mu_result[:], in_=mu_back[:])
-        nc.sync.dma_start(out=out_0[e].rearrange("(p c) s -> p c s", c=ROWS), in_=mu_result[:])
-        sigma_back = psum.tile([P, ROWS, S], F32, tag="mu")
-        transpose_back(e, 1, sigma_back)
-        sigma_result = results.tile([P, ROWS, S], F32, name="sigma_result")
-        nc.scalar.copy(out=sigma_result[:], in_=sigma_back[:])
-        nc.sync.dma_start(out=out_1[e].rearrange("(p c) s -> p c s", c=ROWS), in_=sigma_result[:])
+        first, second = halves
+        last = E - 1
+        regroup_h(last, first)
+        regroup_h(last, second)
+        quantise_h(last, first)
+        add_mu(last - 1, whole)
+        quantise_h(last, second)
+        scale_sigma(last - 1, whole)
+        head_matmuls(last, first)
+        head_matmuls(last, second, "words", "hidden")
+        transpose_back(last - 1, whole)
+        tanh_p(last, first)
+        tanh_p(last, second)
+        store(last - 1, whole, nc.scalar.copy)
+        add_mu(last, first)
+        scale_sigma(last, first)
+        add_mu(last, second)
+        transpose_back(last, first, "p")
+        scale_sigma(last, second)
+        transpose_back(last, second, "mu")
+        store(last, first, nc.vector.tensor_copy)
+        store(last, second, nc.scalar.copy)

@@ -214,27 +214,26 @@ def tile_ensembledynamicmodel_pa_kernel(
                     multiply(sums[:, j, :], w3_mx[e], slice(P * t, P * (t + 1)), h2_mx[e])
                 hidden_sums[e].append(sums)
 
-        def swish(e, cols):
+        def swish(e):
             if not member(e):
                 return
-            width = cols.stop - cols.start
-            planes = work.tile([P, PACK, width], BF16, name="h_planes")
+            planes = work.tile([P, PACK, B], BF16, name="h_planes")
             for t in range(PACK):
                 nc.scalar.activation(
                     out=planes[:, t, :],
-                    in_=hidden_sums[e][t // 2][:, t % 2, cols],
+                    in_=hidden_sums[e][t // 2][:, t % 2, :],
                     func=ACT.Silu,
                     bias=b3_columns[:, PACK * e + t : PACK * e + t + 1],
                     scale=1.0,
                 )
-            h_planes[e, cols.start] = planes
+            h_planes[e] = planes
 
         def regroup_h(e, cols):
             if not member(e):
                 return
             width = cols.stop - cols.start
             grouped = work.tile([P, width, PACK], BF16, name="h_grouped", align_bytes=64)
-            regroup(nc.vector.tensor_copy, grouped[:], h_planes[e, cols.start][:])
+            regroup(nc.vector.tensor_copy, grouped[:], h_planes[e][:, :, cols])
             h_grouped[e, cols.start] = grouped
 
         def quantise_h(e, cols):
@@ -302,14 +301,14 @@ def tile_ensembledynamicmodel_pa_kernel(
                     )
             turned_back[e, cols.start] = back
 
-        def store(e, cols, copy):
+        def store(e, cols, copy, queue=nc.sync):
             if not member(e):
                 return
             rows = slice(cols.start // P, cols.stop // P)
             result = results.tile([P, 2, rows.stop - rows.start, S], F32)
             copy(out=result[:], in_=turned_back[e, cols.start][:])
             for o, out in enumerate((out_0, out_1)):
-                nc.sync.dma_start(
+                queue.dma_start(
                     out=out[e].rearrange("(p c) s -> p c s", c=ROWS)[:, rows, :], in_=result[:, o]
                 )
 
@@ -329,7 +328,7 @@ def tile_ensembledynamicmodel_pa_kernel(
         transpose_h2(2)
         regroup_w3(1)
         regroup_heads(0)
-        swish(0, whole)
+        swish(0)
         copy_h2_words(2)
         spread = psum.tile([P, 1 + ROWS, P], BF16, tag="p")
         nc.tensor.transpose(spread[:, 0, :], small_rows[:], identity_bf16[:])
@@ -377,8 +376,7 @@ def tile_ensembledynamicmodel_pa_kernel(
             scale_sigma(r - 1, whole)
             transpose_back(r - 1, whole)
             regroup_heads(r + 1)
-            for cols in [whole] if r + 1 < E - 1 else halves:
-                swish(r + 1, cols)
+            swish(r + 1)
             copy_h2_words(r + 3)
             quantise_h2(r + 2)
             quantise_h(r, whole)
@@ -410,4 +408,4 @@ def tile_ensembledynamicmodel_pa_kernel(
         scale_sigma(last, second)
         transpose_back(last, second, "mu")
         store(last, first, nc.vector.tensor_copy)
-        store(last, second, nc.scalar.copy)
+        store(last, second, nc.scalar.copy, nc.scalar)

@@ -214,6 +214,13 @@ def tile_ensembledynamicmodel_pa_kernel(
                     multiply(sums[:, j, :], w3_mx[e], slice(P * t, P * (t + 1)), h2_mx[e])
                 hidden_sums[e].append(sums)
 
+        def keep_busy(count):
+            for i in range(count):
+                unread = psum.tile([P, H3], F32, tag="words", bufs=2)
+                nc.tensor.matmul(
+                    unread[:], lhsT=identity_bf16[:], rhs=w3_planes[E - 1][:, i, :], start=True, stop=True
+                )
+
         def swish(e):
             if not member(e):
                 return
@@ -381,8 +388,12 @@ def tile_ensembledynamicmodel_pa_kernel(
             quantise_h2(r + 2)
             quantise_h(r, whole)
             head_matmuls(r, whole)
+            if r + 1 == E - 1:
+                keep_busy(1)
             quantise_w3(r + 2)
             hidden_matmuls(r + 2)
+            if r + 2 == E - 1:
+                keep_busy(2)
             quantise_heads(r + 1)
             tanh_p(r, whole)
             store(r - 1, whole, nc.scalar.copy)

import math
from contextlib import ExitStack

import concourse.mybir as mybir
from concourse.masks import make_identity

F32 = mybir.dt.float32
BF16 = mybir.dt.bfloat16
U32 = mybir.dt.uint32
U8 = mybir.dt.uint8
FP8X4 = mybir.dt.float8_e4m3fn_x4
ACT = mybir.ActivationFunctionType
ALU = mybir.AluOpType

P = 128
PACK = 4
E = 7
B = 256
ROWS = B // P
H2 = 512
H3 = 512
S = 128
RUN = 4

ROW_BMU = 0
ROW_BSIG = ROW_BMU + E
ROW_MAX = ROW_BSIG + E
ROW_MIN = ROW_MAX + 1

FLOPS = 2 * E * B * (H2 * H3 + 2 * H3 * S)


def regroup(copy, grouped, planes):
    copy(
        out=grouped.rearrange("p (m i) t -> p m t i", i=RUN),
        in_=planes.rearrange("p t (m i) -> p m t i", i=RUN),
    )


def tile_ensembledynamicmodel_pa_kernel(
    tc, h2, W3, b3, Wmu, bmu, Wsig, bsig, max_logstd, min_logstd, state, out_0, out_1
):
    nc = tc.nc
    with ExitStack() as ctx:
        const = ctx.enter_context(tc.tile_pool(name="const", bufs=1))
        inputs = ctx.enter_context(tc.tile_pool(name="inputs", bufs=1))
        work = ctx.enter_context(tc.tile_pool(name="work", bufs=3))
        results = ctx.enter_context(tc.tile_pool(name="results", bufs=E + 1))
        psum = ctx.enter_context(tc.psum_pool(name="psum", bufs=1))
        ctx.enter_context(tc.manual_schedule())
        b3_rows = const.tile([P, P], BF16)
        nc.vector.memset(b3_rows[:], 0.0)
        small_rows = const.tile([P, P], BF16)
        nc.vector.memset(small_rows[:], 0.0)
        warm = const.tile([P, 1], F32)
        nc.vector.memset(warm[:], 0.0)
        warm_out = const.tile([P, 1], F32)
        nc.scalar.activation(out=warm_out[:], in_=warm[:], func=ACT.Silu)

        identity = const.tile([P, P], F32)
        make_identity(nc, identity[:])
        identity_bf16 = const.tile([P, P], BF16)
        nc.vector.tensor_copy(out=identity_bf16[:], in_=identity[:])

        h2_rows = {}
        w3_planes = {}
        heads_planes = {}

        def load_h2(e):
            if not 0 <= e < E:
                return
            h2_in = inputs.tile([P, ROWS, H2], BF16, name="h2_rows%d" % e)
            nc.sync.dma_start(out=h2_in[:], in_=h2[e].rearrange("(p c) k -> p c k", c=ROWS))
            h2_rows[e] = h2_in

        def load_w3(e):
            w3_in = inputs.tile([P, PACK, H3], BF16, name="w3_planes%d" % e)
            nc.sync.dma_start(
                out=w3_in[:].rearrange("q (u r) n -> q u (r n)", u=2),
                in_=W3[e].rearrange("(u q r) n -> q u (r n)", u=2, r=2),
            )
            w3_planes[e] = w3_in

        def load_heads(e):
            heads_in = inputs.tile([P, PACK, 2 * S], BF16, name="heads_planes%d" % e)
            nc.sync.dma_start(
                out=heads_in[:, :, 0:S], in_=Wmu[e].rearrange("(t p) s -> p t s", p=P)
            )
            nc.sync.dma_start(
                out=heads_in[:, :, S : 2 * S], in_=Wsig[e].rearrange("(t p) s -> p t s", p=P)
            )
            heads_planes[e] = heads_in

        state_rows = const.tile([P, ROWS, S], BF16)
        load_h2(0)
        load_w3(0)
        nc.sync.dma_start(out=b3_rows[0 : E * PACK, :], in_=b3.rearrange("e (t p) -> (e t) p", p=P))
        nc.sync.dma_start(
            out=small_rows[ROW_MAX:ROW_MIN, :], in_=max_logstd.rearrange("(o s) -> o s", o=1)
        )
        nc.sync.dma_start(
            out=small_rows[ROW_MIN : ROW_MIN + 1, :], in_=min_logstd.rearrange("(o s) -> o s", o=1)
        )
        load_h2(1)
        load_w3(1)
        nc.sync.dma_start(out=small_rows[ROW_BMU:ROW_BSIG, :], in_=bmu)
        nc.sync.dma_start(out=small_rows[ROW_BSIG:ROW_MAX, :], in_=bsig)
        load_heads(0)
        nc.sync.dma_start(out=state_rows[:], in_=state.rearrange("(p c) s -> p c s", c=ROWS))
        load_h2(2)
        for e in range(2, E):
            load_w3(e)
            load_heads(e - 1)
            load_h2(e + 1)
        load_heads(E - 1)

        h2_words = {}
        h2_grouped = {}
        h2_mx = {}
        w3_grouped = {}
        w3_mx = {}
        heads_grouped = {}
        heads_mx = {}
        hidden_sums = {}
        h_planes = {}
        h_grouped = {}
        tanhs = {}
        h_mx = {}
        head_sums = {}
        turned = {}
        turned_back = {}

        def quantise(grouped, width, label):
            codes = work.tile([P, width], U32, name=label + "_codes", align_bytes=64)
            scales = work.tile([P, width], U8, name=label + "_scales", align_bytes=64)
            nc.vector.quantize_mx(
                out=codes[:].bitcast(FP8X4),
                scales=scales[:],
                in_=grouped[:].rearrange("p w t -> p (w t)"),
            )
            return codes, scales

        def multiply(out, stationary, chunk, moving):
            nc.tensor.matmul_mx(
                out=out,
                lhsT=stationary[0][:, chunk].bitcast(FP8X4),
                lhsT_scale=stationary[1][:, chunk],
                rhs=moving[0][:].bitcast(FP8X4),
                rhs_scale=moving[1][:],
                start=True,
                stop=True,
            )

        def member(e):
            return 0 <= e < E

        whole = slice(0, B)
        halves = [slice(0, P), slice(P, B)]

        def transpose_h2(e):
            if not member(e):
                return
            words = h2_rows[e][:].bitcast(F32)
            h2_t = psum.tile([P, 2, ROWS, P], F32, tag="words", bufs=2)
            for u in range(2):
                for c in range(ROWS):
                    nc.tensor.transpose(h2_t[:, u, c, :], words[:, c, P * u : P * (u + 1)], identity[:])
            h2_words[e] = h2_t

        def copy_h2_words(e):
            if not member(e):
                return
            grouped = work.tile([P, B, PACK], BF16, name="h2_grouped", align_bytes=64)
            nc.scalar.copy(
                out=grouped[:].bitcast(F32), in_=h2_words[e][:].rearrange("q u c p -> q (c p) u")
            )
            h2_grouped[e] = grouped

        def regroup_w3(e):
            if not member(e):
                return
            grouped = work.tile([P, H3, PACK], BF16, name="w3_grouped", align_bytes=64)
            regroup(nc.vector.tensor_copy, grouped[:], w3_planes[e][:])
            w3_grouped[e] = grouped

        def regroup_heads(e):
            if not member(e):
                return
            grouped = work.tile([P, 2 * S, PACK], BF16, name="heads_grouped", align_bytes=64)
            copy = nc.scalar.copy if e < E - 1 else nc.vector.tensor_copy
            regroup(copy, grouped[:], heads_planes[e][:])
            heads_grouped[e] = grouped

        def quantise_h2(e):
            if member(e):
                h2_mx[e] = quantise(h2_grouped[e], B, "h2")

        def quantise_w3(e):
            if member(e):
                w3_mx[e] = quantise(w3_grouped[e], H3, "w3")

        def quantise_heads(e):
            if member(e):
                heads_mx[e] = quantise(heads_grouped[e], 2 * S, "heads")

        def hidden_matmuls(e):
            if not member(e):
                return
            hidden_sums[e] = []
            for half in range(2):
                sums = psum.tile([P, 2, B], F32, tag="hidden", bufs=3)
                for j in range(2):
                    t = 2 * half + j
                    multiply(sums[:, j, :], w3_mx[e], slice(P * t, P * (t + 1)), h2_mx[e])
                hidden_sums[e].append(sums)

        def keep_busy(count):
            for i in range(count):
                unread = psum.tile([P, H3], F32, tag="words", bufs=2)
                nc.tensor.matmul(
                    unread[:], lhsT=identity_bf16[:], rhs=w3_planes[E - 1][:, i, :], start=True, stop=True
                )

        def swish(e):
            if not member(e):
                return
            planes = work.tile([P, PACK, B], BF16, name="h_planes")
            for t in range(PACK):
                nc.scalar.activation(
                    out=planes[:, t, :],
                    in_=hidden_sums[e][t // 2][:, t % 2, :],
                    func=ACT.Silu,
                    bias=b3_columns[:, PACK * e + t : PACK * e + t + 1],
                    scale=1.0,
                )
            h_planes[e] = planes

        def regroup_h(e, cols):
            if not member(e):
                return
            width = cols.stop - cols.start
            grouped = work.tile([P, width, PACK], BF16, name="h_grouped", align_bytes=64)
            regroup(nc.vector.tensor_copy, grouped[:], h_planes[e][:, :, cols])
            h_grouped[e, cols.start] = grouped

        def quantise_h(e, cols):
            if member(e):
                h_mx[e, cols.start] = quantise(h_grouped[e, cols.start], cols.stop - cols.start, "h")

        def head_matmuls(e, cols, p_tag="p", mu_tag="mu"):
            if not member(e):
                return
            width = cols.stop - cols.start
            p_sums = psum.tile([P, width], F32, tag=p_tag, bufs=2 if p_tag == "words" else 1)
            multiply(p_sums[:], heads_mx[e], slice(S, 2 * S), h_mx[e, cols.start])
            mu_sums = psum.tile([P, width], F32, tag=mu_tag, bufs=3 if mu_tag == "hidden" else 1)
            multiply(mu_sums[:], heads_mx[e], slice(0, S), h_mx[e, cols.start])
            head_sums[e, cols.start] = (mu_sums, p_sums)

        def add_mu(e, cols):
            if not member(e):
                return
            both = work.tile([P, 2, cols.stop - cols.start], F32, name="both")
            nc.vector.scalar_tensor_tensor(
                out=both[:, 0, :],
                in0=head_sums[e, cols.start][0][:],
                scalar=columns[:, ROW_BMU + e : ROW_BMU + e + 1],
                in1=state_t[:, cols],
                op0=ALU.add,
                op1=ALU.add,
            )
            turned[e, cols.start] = both

        def tanh_p(e, cols):
            if not member(e):
                return
            tanh = work.tile([P, cols.stop - cols.start], F32, name="tanh")
            nc.scalar.activation(
                out=tanh[:],
                in_=head_sums[e, cols.start][1][:],
                func=ACT.Tanh,
                bias=tanh_bias[:, e : e + 1],
                scale=0.5,
            )
            tanhs[e, cols.start] = tanh

        def scale_sigma(e, cols):
            if not member(e):
                return
            nc.vector.tensor_scalar(
                out=turned[e, cols.start][:, 1, :],
                in0=tanhs[e, cols.start][:],
                scalar1=sigma_affine[:, 0:1],
                scalar2=sigma_affine[:, 1:2],
                op0=ALU.mult,
                op1=ALU.add,
            )

        def transpose_back(e, cols, tag="back"):
            if not member(e):
                return
            rows = (cols.stop - cols.start) // P
            back = psum.tile([P, 2, rows, S], F32, tag=tag)
            for o in range(2):
                for c in range(rows):
                    nc.tensor.transpose(
                        back[:, o, c, :], turned[e, cols.start][:, o, P * c : P * (c + 1)], identity[:]
                    )
            turned_back[e, cols.start] = back

        def store(e, cols, copy, queue=nc.sync):
            if not member(e):
                return
            rows = slice(cols.start // P, cols.stop // P)
            result = results.tile([P, 2, rows.stop - rows.start, S], F32)
            copy(out=result[:], in_=turned_back[e, cols.start][:])
            for o, out in enumerate((out_0, out_1)):
                queue.dma_start(
                    out=out[e].rearrange("(p c) s -> p c s", c=ROWS)[:, rows, :], in_=result[:, o]
                )

        transpose_h2(0)
        copy_h2_words(0)
        regroup_w3(0)
        b3_spread = psum.tile([P, P], BF16, tag="back")
        nc.tensor.transpose(b3_spread[:], b3_rows[:], identity_bf16[:])
        transpose_h2(1)
        quantise_h2(0)
        quantise_w3(0)
        b3_columns = const.tile([P, P], F32)
        nc.vector.tensor_copy(out=b3_columns[:], in_=b3_spread[:])
        copy_h2_words(1)
        hidden_matmuls(0)

        transpose_h2(2)
        regroup_w3(1)
        regroup_heads(0)
        swish(0)
        copy_h2_words(2)
        spread = psum.tile([P, 1 + ROWS, P], BF16, tag="p")
        nc.tensor.transpose(spread[:, 0, :], small_rows[:], identity_bf16[:])
        for c in range(ROWS):
            nc.tensor.transpose(spread[:, 1 + c, :], state_rows[:, c, :], identity_bf16[:])
        quantise_h2(1)
        quantise_w3(1)
        hidden_matmuls(1)
        quantise_heads(0)

        for r in range(E - 1):
            transpose_h2(r + 3)
            regroup_w3(r + 2)
            if r == 0:
                columns = const.tile([P, P], F32)
                nc.vector.tensor_copy(out=columns[:], in_=spread[:, 0, :])
                state_t = const.tile([P, B], BF16)
                nc.vector.tensor_copy(out=state_t[:], in_=spread[:, 1:, :].rearrange("s c p -> s (c p)"))
                base = const.tile([P, 2], F32)
                nc.gpsimd.tensor_scalar(
                    out=base[:], in0=columns[:, ROW_MAX : ROW_MIN + 1], scalar1=0.0, scalar2=math.e, op0=ALU.mult, op1=ALU.add
                )
                exp_bounds = const.tile([P, 2], F32)
                nc.gpsimd.tensor_tensor(
                    out=exp_bounds[:], in0=base[:], in1=columns[:, ROW_MAX : ROW_MIN + 1], op=ALU.pow
                )
                tanh_bias = const.tile([P, E], F32)
                nc.gpsimd.tensor_scalar(
                    out=tanh_bias[:],
                    in0=columns[:, ROW_BSIG:ROW_MAX],
                    scalar1=columns[:, ROW_MAX : ROW_MAX + 1],
                    scalar2=0.5,
                    op0=ALU.subtract,
                    op1=ALU.mult,
                )
                sigma_affine = const.tile([P, 2], F32)
                nc.gpsimd.tensor_scalar(
                    out=sigma_affine[:, 0:1], in0=exp_bounds[:, 0:1], scalar1=0.5, scalar2=0.0, op0=ALU.mult, op1=ALU.add
                )
                nc.gpsimd.tensor_tensor(
                    out=sigma_affine[:, 1:2], in0=sigma_affine[:, 0:1], in1=exp_bounds[:, 1:2], op=ALU.add
                )
            regroup_h(r, whole)
            add_mu(r - 1, whole)
            scale_sigma(r - 1, whole)
            transpose_back(r - 1, whole)
            regroup_heads(r + 1)
            swish(r + 1)
            copy_h2_words(r + 3)
            quantise_h2(r + 2)
            quantise_h(r, whole)
            head_matmuls(r, whole)
            if r + 1 == E - 1:
                keep_busy(1)
            quantise_w3(r + 2)
            hidden_matmuls(r + 2)
            if r + 2 == E - 1:
                keep_busy(2)
            quantise_heads(r + 1)
            tanh_p(r, whole)
            store(r - 1, whole, nc.scalar.copy)

        first, second = halves
        last = E - 1
        regroup_h(last, first)
        regroup_h(last, second)
        quantise_h(last, first)
        add_mu(last - 1, whole)
        quantise_h(last, second)
        scale_sigma(last - 1, whole)
        head_matmuls(last, first)
        head_matmuls(last, second, "words", "hidden")
        transpose_back(last - 1, whole)
        tanh_p(last, first)
        tanh_p(last, second)
        store(last - 1, whole, nc.scalar.copy)
        add_mu(last, first)
        scale_sigma(last, first)
        add_mu(last, second)
        transpose_back(last, first, "p")
        scale_sigma(last, second)
        transpose_back(last, second, "mu")
        store(last, first, nc.vector.tensor_copy)
        store(last, second, nc.scalar.copy, nc.scalar)
